import numpy as np
import ml_dtypes


def mxq(x, axis, fmt="e4m3"):
    dtype, down = {"e4m3": (ml_dtypes.float8_e4m3fn, 7), "e5m2": (ml_dtypes.float8_e5m2, 14)}[fmt]
    v = np.moveaxis(np.asarray(x, np.float32).astype(ml_dtypes.bfloat16).astype(np.float64), axis, -1)
    blocks = v.reshape(v.shape[:-1] + (-1, 32))
    amax = np.abs(blocks).max(-1, keepdims=True)
    byte = np.maximum(np.where(amax > 0, np.frexp(amax)[1] - 1 + 127, 0) - down, 1)
    scale = np.exp2(byte - 127.0)
    codes = (blocks / scale).astype(np.float32).astype(dtype).astype(np.float64)
    return np.moveaxis((codes * scale).reshape(v.shape), -1, axis)


WIDE = False


def mx_kscale(k):
    if not WIDE:
        return np.ones(k)
    levels = np.array([10, -10, 5, -5, 0])
    if k % 512:
        return np.exp2(np.random.permutation(np.resize(levels, k // 32))).repeat(32)
    a = np.empty((k // 512, 16))
    for p in range(k // 512):
        a[p, :8] = np.random.permutation(np.resize(levels, 8))
        for g in range(8):
            far = levels[np.abs(levels - a[p, g]) >= 10]
            a[p, g + 8] = far[np.random.randint(len(far))]
    return np.exp2(a.ravel()).repeat(32)


BF16 = ml_dtypes.bfloat16


def bf(x):
    return np.asarray(x, np.float32).astype(BF16)


def f64(x):
    return np.asarray(x).astype(np.float64)


B, L, D, O = 16, 256, 512, 2


def draw0():
    s = mx_kscale(D)
    u = mx_kscale(D)
    w = np.random.standard_normal((O, D + 1, D))
    w[:, :D, :] *= 3.0 / D / s[:, None]
    w[:, D, :] *= 1.0 / np.sqrt(D)
    return {"x1": bf(np.random.standard_normal((B, L, D)) * s),
            "x2": bf(np.random.standard_normal((B, L, D)) / u),
            "bw": bf(np.random.uniform(size=(2,))),
            "W_bil": bf(w * u),
            "t_ones": bf(np.random.standard_normal((B, L, O))),
            "lin1": bf(np.random.standard_normal((B, L, O))),
            "lin2": bf(np.random.standard_normal((B, L, O))),
            "b_lin": bf(np.random.standard_normal(O) * 0.5)}


def core(x1, x2, bw, W_bil, t_ones, lin1, lin2, b_lin):
    e = np.exp(f64(bw) - f64(bw).max())
    bwn = e / e.sum()
    w = f64(W_bil)
    t = (mxq(f64(x1).reshape(B * L, D), 1, "e4m3") @ mxq(w[:, :D, :], 1, "e4m3")) + w[:, D, :][:, None, :]
    t = t.reshape(O, B, L, D)
    pair = mxq(t, 3, "e4m3") @ mxq(f64(x2), 2, "e4m3").transpose(0, 2, 1)
    bil = pair.transpose(1, 2, 3, 0) + f64(t_ones)[:, :, None, :]
    lin = f64(lin1)[:, :, None, :] + f64(lin2)[:, None, :, :] + f64(b_lin)
    return bwn[0] * bil + bwn[1] * lin


def e4m3fn_bytes(y):
    return np.clip(np.asarray(y, np.float64), -448.0, 448.0).astype(np.float32).astype(ml_dtypes.float8_e4m3fn).view(np.uint8)


def e4m3fn_values(b):
    return np.asarray(b, np.uint8).view(ml_dtypes.float8_e4m3fn).astype(np.float64)


def setup_inputs():
    d = draw0()
    x0 = np.asarray(d['x2']).astype(np.float64)
    s = (np.max(np.abs(x0), axis=(0, 1), keepdims=True) / 448.0).astype(np.float32)
    out = {}
    for k, v in d.items():
        if k == 'x2':
            out['x2_bytes'] = e4m3fn_bytes(x0 / s.astype(np.float64))
            out['x2_scale'] = s
        else:
            out[k] = v
    return out


def reference(x1, x2_bytes, x2_scale, bw, W_bil, t_ones, lin1, lin2, b_lin):
    return core(x1, e4m3fn_values(x2_bytes) * x2_scale.astype(np.float64), bw, W_bil, t_ones, lin1, lin2, b_lin)

@@ -1,0 +1,305 @@
+from contextlib import ExitStack
+
+import concourse.mybir as mybir
+from concourse.masks import make_identity
+
+B, L, D, O = 16, 256, 512, 2
+FLOPS = 2 * D * (B * L) * (D * O) + 2 * B * L * L * D * O
+
+F32 = mybir.dt.float32
+BF16 = mybir.dt.bfloat16
+U32 = mybir.dt.uint32
+U8 = mybir.dt.uint8
+FP8 = mybir.dt.float8_e4m3fn
+FP8X4 = mybir.dt.float8_e4m3fn_x4
+ACT = mybir.ActivationFunctionType
+ALU = mybir.AluOpType
+AX = mybir.AxisListType
+
+P = 128
+LIN_GROUP = 4
+
+
+def tile_biaffine_pa_t_kernel(tc, x1, x2_bytes, x2_scale, bw, W_bil, t_ones, lin1, lin2, b_lin, out):
+    nc = tc.nc
+    with ExitStack() as ctx:
+        keep = ctx.enter_context(tc.tile_pool(name="keep", bufs=1))
+        loads = ctx.enter_context(tc.tile_pool(name="loads", bufs=B))
+        work = ctx.enter_context(tc.tile_pool(name="work", bufs=3))
+        ps_tr = ctx.enter_context(tc.psum_pool(name="ps_tr", bufs=1))
+        ps_t = ctx.enter_context(tc.psum_pool(name="ps_t", bufs=4))
+        ps_o = ctx.enter_context(tc.psum_pool(name="ps_o", bufs=2))
+        ctx.enter_context(tc.manual_schedule())
+
+        w_raw = []
+        for o in range(O):
+            w_raw.append(keep.tile([P, 4, D], BF16, name=f"w_raw{o}", align_bytes=64))
+        x1_sb, x2_sb = {}, {}
+
+        def load_w(o):
+            nc.sync.dma_start(out=w_raw[o][:], in_=W_bil[o, 0:D, :].rearrange("(p t) j -> p t j", t=4))
+
+        def load_x1(b):
+            x1_sb[b] = loads.tile([P, 2, D], BF16, name="x1_rows", align_bytes=64)
+            nc.sync.dma_start(out=x1_sb[b][:], in_=x1[b].rearrange("(p x) k -> p x k", x=2))
+
+        def load_x2(b):
+            x2_sb[b] = loads.tile([P, 2, D], U8, name="x2_codes_in", align_bytes=64)
+            nc.sync.dma_start(out=x2_sb[b][:], in_=x2_bytes[b].rearrange("(y p) k -> p y k", y=2))
+
+        lin2_sb = {}
+
+        def load_lin2(g):
+            lin2_sb[g] = keep.tile([P, LIN_GROUP, L * O], BF16, name=f"lin2_{g}", align_bytes=64)
+            nc.sync.dma_start(
+                out=lin2_sb[g][:].rearrange("p b c -> p (b c)"),
+                in_=lin2[g * LIN_GROUP : (g + 1) * LIN_GROUP].rearrange("b y o -> (b y o)").partition_broadcast(P),
+            )
+
+        load_w(0)
+        load_x1(0)
+        load_w(1)
+        load_x2(0)
+        load_x1(1)
+        load_x2(1)
+        load_x1(2)
+        load_x2(2)
+        load_lin2(0)
+        for b in range(3, B):
+            load_x1(b)
+            load_x2(b)
+            if b % LIN_GROUP == 1:
+                load_lin2(b // LIN_GROUP)
+
+        bw_sb = keep.tile([P, 2], BF16, name="bw_sb")
+        nc.scalar.dma_start(out=bw_sb[:], in_=bw.partition_broadcast(P))
+        scale_sb = keep.tile([P, 4], F32, name="scale_sb")
+        nc.scalar.dma_start(out=scale_sb[:], in_=x2_scale.rearrange("a c (p t) -> p (a c t)", t=4))
+        bias_bf = keep.tile([P, O, 4], BF16, name="bias_bf")
+        nc.scalar.dma_start(out=bias_bf[:], in_=W_bil[:, D, :].rearrange("o (p t) -> p o t", t=4))
+        blin_sb = keep.tile([P, 2], BF16, name="blin_sb")
+        nc.scalar.dma_start(out=blin_sb[:], in_=b_lin.partition_broadcast(P))
+        rows = keep.tile([P, L * O], BF16, name="rows")
+        nc.gpsimd.memset(rows[:], 0.0)
+        nc.scalar.dma_start(out=rows[0:B, :], in_=t_ones.rearrange("b x o -> b (x o)"))
+        nc.scalar.dma_start(out=rows[32 : 32 + B, :], in_=lin1.rearrange("b x o -> b (x o)"))
+
+        ident = keep.tile([P, P], F32, name="ident")
+        make_identity(nc, ident[:])
+
+        bw_max = keep.tile([P, 1], F32, name="bw_max")
+        nc.vector.reduce_max(bw_max[:], bw_sb[:], axis=AX.X)
+        bw_dif = keep.tile([P, 2], F32, name="bw_dif")
+        nc.vector.tensor_scalar(out=bw_dif[:], in0=bw_sb[:], scalar1=bw_max[:], scalar2=None, op0=ALU.subtract)
+        bw_exp = keep.tile([P, 2], F32, name="bw_exp")
+        nc.scalar.activation(out=bw_exp[:], in_=bw_dif[:], func=ACT.Exp)
+        bw_sum = keep.tile([P, 1], F32, name="bw_sum")
+        nc.vector.reduce_sum(bw_sum[:], bw_exp[:], axis=AX.X)
+        bw_inv = keep.tile([P, 1], F32, name="bw_inv")
+        nc.vector.reciprocal(out=bw_inv[:], in_=bw_sum[:])
+        bwn = keep.tile([P, 2], F32, name="bwn")
+        nc.vector.tensor_scalar(out=bwn[:], in0=bw_exp[:], scalar1=bw_inv[:], scalar2=None, op0=ALU.mult)
+        bias = keep.tile([P, O * 4], F32, name="bias")
+        nc.vector.tensor_copy(out=bias[:], in_=bias_bf[:].rearrange("p o t -> p (o t)"))
+
+        w_codes, w_scales = [], []
+        w_grp = []
+        for o in range(O):
+            w_grp.append(keep.tile([P, D * 4], BF16, name=f"w_grp{o}", align_bytes=64))
+            w_codes.append(keep.tile([P, D], U32, name=f"w_codes{o}", align_bytes=64))
+            w_scales.append(keep.tile([P, D], U8, name=f"w_scales{o}", align_bytes=64))
+
+        def w_group(o, copy):
+            for t in range(4):
+                copy(
+                    out=w_grp[o][:].rearrange("p (t m j) -> p t m j", t=4, j=4)[:, t],
+                    in_=w_raw[o][:].rearrange("p j (m t) -> p t m j", t=4)[:, t],
+                )
+
+        def w_quant(o):
+            nc.vector.quantize_mx(out=w_codes[o][:].bitcast(FP8X4), scales=w_scales[o][:], in_=w_grp[o][:])
+
+        x2_bf, x1_tr, x2_tr, x_grp = {}, {}, {}, {}
+        x_c, x_s, t_bank, t_pl, t_grp, t_c, t_s, o_bank, ra, o_sb = {}, {}, {}, {}, {}, {}, {}, {}, {}, {}
+
+        def cast_x2(b):
+            x2_bf[b] = work.tile([P, 2, D], BF16, name="x2_bf", align_bytes=64)
+            nc.scalar.copy(out=x2_bf[b][:], in_=x2_sb[b][:].bitcast(FP8))
+
+        def transpose_rows(src, dst):
+            words = src[:].rearrange("p x k -> p (x k)").bitcast(F32)
+            for x in range(2):
+                for u in range(2):
+                    nc.tensor.transpose(
+                        dst[:, (2 * u + x) * P : (2 * u + x + 1) * P],
+                        words[:, x * 256 + u : (x + 1) * 256 : 2],
+                        ident[:],
+                    )
+
+        def tr_x1(b):
+            x1_tr[b] = ps_tr.tile([P, 512], F32, name="x1_tr")
+            transpose_rows(x1_sb[b], x1_tr[b])
+
+        def tr_x2(b):
+            x2_tr[b] = ps_tr.tile([P, 512], F32, name="x2_tr")
+            transpose_rows(x2_bf[b], x2_tr[b])
+
+        def evac_x1(b):
+            x_grp[b] = work.tile([P, 2 * L * 4], BF16, name="x_grp", align_bytes=64)
+            nc.scalar.copy(
+                out=x_grp[b][:, 0 : L * 4].bitcast(F32).rearrange("p (c u) -> p c u", u=2),
+                in_=x1_tr[b][:].rearrange("p (u c) -> p c u", u=2),
+            )
+
+        def quant_x(b, lo, hi):
+            x_c[b] = work.tile([P, 2 * L], U32, name="x_c", align_bytes=64)
+            x_s[b] = work.tile([P, 2 * L], U8, name="x_s", align_bytes=64)
+            nc.vector.quantize_mx(out=x_c[b][:, lo:hi].bitcast(FP8X4), scales=x_s[b][:, lo:hi], in_=x_grp[b][:, 4 * lo : 4 * hi])
+
+        def quant_t(b):
+            t_c[b] = work.tile([P, 2 * L], U32, name="t_c", align_bytes=64)
+            t_s[b] = work.tile([P, 2 * L], U8, name="t_s", align_bytes=64)
+            nc.vector.quantize_mx(out=t_c[b][:].bitcast(FP8X4), scales=t_s[b][:], in_=t_grp[b][:])
+
+        def scale_x2(b):
+            src = x2_tr[b][:].bitcast(BF16).rearrange("p (u c e) -> p c u e", u=2, e=2)
+            dst = x_grp[b + 1][:, L * 4 :].rearrange("p (c u e) -> p c u e", u=2, e=2)
+            sc = scale_sb[:].rearrange("p (u e) -> p u e", e=2).unsqueeze(1).to_broadcast([P, L, 2, 2])
+            nc.vector.tensor_tensor(out=dst, in0=src, in1=sc, op=ALU.mult)
+
+        def mm_t(b):
+            t_pl[b] = work.tile([P, 4, O * L], BF16, name="t_pl", align_bytes=64)
+            for o in range(O):
+                for h in range(2):
+                    bank = ps_t.tile([P, 512], F32, name="t_bank")
+                    t_bank[b, o, h] = bank
+                    for t in (2 * h, 2 * h + 1):
+                        nc.tensor.matmul_mx(
+                            out=bank[:, (t % 2) * L : (t % 2 + 1) * L],
+                            lhsT=w_codes[o][:, t * P : (t + 1) * P].bitcast(FP8X4),
+                            lhsT_scale=w_scales[o][:, t * P : (t + 1) * P],
+                            rhs=x_c[b][:, 0:L].bitcast(FP8X4),
+                            rhs_scale=x_s[b][:, 0:L],
+                            start=True,
+                            stop=True,
+                        )
+
+        def evac_t(b):
+            for o in range(O):
+                for t in range(4):
+                    nc.scalar.activation(
+                        out=t_pl[b][:, t, o * L : (o + 1) * L],
+                        in_=t_bank[b, o, t // 2][:, (t % 2) * L : (t % 2 + 1) * L],
+                        func=ACT.Identity,
+                        bias=bias[:, o * 4 + t : o * 4 + t + 1],
+                    )
+
+        def inter_t(b):
+            t_grp[b] = work.tile([P, O * L * 4], BF16, name="t_grp", align_bytes=64)
+            nc.vector.tensor_copy(
+                out=t_grp[b][:].rearrange("p (c i t) -> p c t i", i=4, t=4),
+                in_=t_pl[b][:].rearrange("p t (c i) -> p c t i", i=4),
+            )
+
+        def mm_out(b):
+            for x in range(2):
+                o_bank[b, x] = ps_o.tile([P, 512], F32, name="o_bank")
+                for o in range(O):
+                    nc.tensor.matmul_mx(
+                        out=o_bank[b, x][:, o * L : (o + 1) * L],
+                        lhsT=t_c[b][:, o * L + x * P : o * L + (x + 1) * P].bitcast(FP8X4),
+                        lhsT_scale=t_s[b][:, o * L + x * P : o * L + (x + 1) * P],
+                        rhs=x_c[b + 1][:, L : 2 * L].bitcast(FP8X4),
+                        rhs_scale=x_s[b + 1][:, L : 2 * L],
+                        start=True,
+                        stop=True,
+                    )
+
+        def terms(b):
+            ra[b] = work.tile([P, 2, O, L], F32, name="ra", align_bytes=64)
+            l2 = lin2_sb[b // LIN_GROUP][:, b % LIN_GROUP, :].rearrange("p (y o) -> p o y", o=2)
+            for x in range(2):
+                for o in range(O):
+                    i = (x * B + b) * O + o
+                    nc.gpsimd.tensor_scalar(
+                        out=ra[b][:, x, o, :], in0=l2[:, o, :], scalar1=bwn[:, 1:2], scalar2=a_sb[:, i : i + 1], op0=ALU.mult, op1=ALU.add
+                    )
+
+        def finish(b, x):
+            if x == 0:
+                o_sb[b] = work.tile([P, 2, L * O], F32, name="o_sb", align_bytes=64)
+            nc.vector.scalar_tensor_tensor(
+                out=o_sb[b][:, x, :].rearrange("p (y o) -> p y o", o=2),
+                in0=o_bank[b, x][:].rearrange("p (o y) -> p y o", o=2),
+                scalar=bwn[:, 0:1],
+                in1=ra[b][:, x].rearrange("p o y -> p y o"),
+                op0=ALU.mult,
+                op1=ALU.add,
+            )
+            dst = out[b].rearrange("(p x) y o -> p x (y o)", x=2)
+            if b == B - 1:
+                nc.sync.dma_start(out=dst[:, x, :], in_=o_sb[b][:, x, :])
+            elif x == 1:
+                nc.sync.dma_start(out=dst, in_=o_sb[b][:])
+
+        a_tr = ps_o.tile([P, 512], F32, name="o_bank")
+        a_words = rows[:].bitcast(F32)
+        for x in range(2):
+            nc.tensor.transpose(a_tr[:, x * P : (x + 1) * P], a_words[:, x::2], ident[:])
+        a_sb = keep.tile([P, 2 * B * O], F32, name="a_sb")
+        a_tmp = keep.tile([P, 2 * B * O], F32, name="a_tmp")
+        a_view = a_tr[:, 0 : 2 * P].bitcast(BF16).rearrange("p (x w o) -> p x w o", x=2, o=2)
+        tmp_v = a_tmp[:].rearrange("p (x b o) -> p x b o", x=2, o=2)
+        blin_v = blin_sb[:].unsqueeze(1).to_broadcast([P, B, O])
+
+        w_group(0, nc.vector.tensor_copy)
+        tr_x1(0)
+        evac_x1(0)
+        w_quant(0)
+        cast_x2(0)
+        w_group(1, nc.scalar.copy)
+        quant_x(0, 0, L)
+        for x in range(2):
+            nc.vector.tensor_tensor(out=tmp_v[:, x], in0=a_view[:, x, 32 : 32 + B], in1=blin_v, op=ALU.add)
+        nc.vector.tensor_scalar(out=a_tmp[:], in0=a_tmp[:], scalar1=bwn[:, 1:2], scalar2=None, op0=ALU.mult)
+        w_quant(1)
+        for x in range(2):
+            nc.vector.scalar_tensor_tensor(
+                out=a_sb[:].rearrange("p (x b o) -> p x b o", x=2, o=2)[:, x],
+                in0=a_view[:, x, 0:B], scalar=bwn[:, 0:1], in1=tmp_v[:, x], op0=ALU.mult, op1=ALU.add,
+            )
+        terms(0)
+        tr_x1(1)
+        tr_x2(0)
+        evac_x1(1)
+        cast_x2(1)
+
+        for s in range(B + 1):
+            if s < B:
+                mm_t(s)
+            if s >= 1:
+                mm_out(s - 1)
+            if s + 2 < B:
+                tr_x1(s + 2)
+            if s < B:
+                evac_t(s)
+            if s + 2 < B:
+                evac_x1(s + 2)
+                cast_x2(s + 2)
+            if s + 1 < B:
+                terms(s + 1)
+            if s == B - 1:
+                x_grp[B] = work.tile([P, 2 * L * 4], BF16, name="x_grp", align_bytes=64)
+            if s < B:
+                scale_x2(s)
+            if s + 1 < B:
+                tr_x2(s + 1)
+            if s >= 1:
+                finish(s - 1, 0)
+            if s < B:
+                quant_x(s + 1, L if s == B - 1 else 0, 2 * L)
+                inter_t(s)
+            if s >= 1:
+                finish(s - 1, 1)
+            if s < B:
+                quant_t(s)

@@ -18,6 +18,7 @@ AX = mybir.AxisListType
 
 P = 128
 LIN_GROUP = 4
+S_COLS = 128
 
 
 def tile_biaffine_pa_t_kernel(tc, x1, x2_bytes, x2_scale, bw, W_bil, t_ones, lin1, lin2, b_lin, out):
@@ -56,8 +57,8 @@ def tile_biaffine_pa_t_kernel(tc, x1, x2_bytes, x2_scale, bw, W_bil, t_ones, lin
                 in_=lin2[g * LIN_GROUP : (g + 1) * LIN_GROUP].rearrange("b y o -> (b y o)").partition_broadcast(P),
             )
 
-        load_w(0)
         load_x1(0)
+        load_w(0)
         load_w(1)
         load_x2(0)
         load_x1(1)
@@ -123,7 +124,7 @@ def tile_biaffine_pa_t_kernel(tc, x1, x2_bytes, x2_scale, bw, W_bil, t_ones, lin
         x_c, x_s, t_bank, t_pl, t_grp, t_c, t_s, o_bank, ra, o_sb = {}, {}, {}, {}, {}, {}, {}, {}, {}, {}
 
         def cast_x2(b):
-            x2_bf[b] = work.tile([P, 2, D], BF16, name="x2_bf", align_bytes=64)
+            x2_bf[b] = work.tile([P, 2, D], BF16, name="x2_bf", bufs=4, align_bytes=64)
             nc.scalar.copy(out=x2_bf[b][:], in_=x2_sb[b][:].bitcast(FP8))
 
         def transpose_rows(src, dst):
@@ -152,8 +153,9 @@ def tile_biaffine_pa_t_kernel(tc, x1, x2_bytes, x2_scale, bw, W_bil, t_ones, lin
             )
 
         def quant_x(b, lo, hi):
-            x_c[b] = work.tile([P, 2 * L], U32, name="x_c", align_bytes=64)
-            x_s[b] = work.tile([P, 2 * L], U8, name="x_s", align_bytes=64)
+            if lo == 0:
+                x_c[b] = work.tile([P, 2 * L], U32, name="x_c", bufs=4, align_bytes=64)
+                x_s[b] = work.tile([P, 2 * L], U8, name="x_s", bufs=4, align_bytes=64)
             nc.vector.quantize_mx(out=x_c[b][:, lo:hi].bitcast(FP8X4), scales=x_s[b][:, lo:hi], in_=x_grp[b][:, 4 * lo : 4 * hi])
 
         def quant_t(b):
@@ -163,13 +165,14 @@ def tile_biaffine_pa_t_kernel(tc, x1, x2_bytes, x2_scale, bw, W_bil, t_ones, lin
 
         def scale_x2(b):
             src = x2_tr[b][:].bitcast(BF16).rearrange("p (u c e) -> p c u e", u=2, e=2)
-            dst = x_grp[b + 1][:, L * 4 :].rearrange("p (c u e) -> p c u e", u=2, e=2)
+            dst = x_grp[b][:, L * 4 :].rearrange("p (c u e) -> p c u e", u=2, e=2)
             sc = scale_sb[:].rearrange("p (u e) -> p u e", e=2).unsqueeze(1).to_broadcast([P, L, 2, 2])
             nc.vector.tensor_tensor(out=dst, in0=src, in1=sc, op=ALU.mult)
 
-        def mm_t(b):
-            t_pl[b] = work.tile([P, 4, O * L], BF16, name="t_pl", align_bytes=64)
-            for o in range(O):
+        def mm_t(b, o):
+            if o == 0:
+                t_pl[b] = work.tile([P, 4, O * L], BF16, name="t_pl", align_bytes=64)
+            if True:
                 for h in range(2):
                     bank = ps_t.tile([P, 512], F32, name="t_bank")
                     t_bank[b, o, h] = bank
@@ -184,8 +187,8 @@ def tile_biaffine_pa_t_kernel(tc, x1, x2_bytes, x2_scale, bw, W_bil, t_ones, lin
                             stop=True,
                         )
 
-        def evac_t(b):
-            for o in range(O):
+        def evac_t(b, o):
+            if True:
                 for t in range(4):
                     nc.scalar.activation(
                         out=t_pl[b][:, t, o * L : (o + 1) * L],
@@ -194,11 +197,20 @@ def tile_biaffine_pa_t_kernel(tc, x1, x2_bytes, x2_scale, bw, W_bil, t_ones, lin
                         bias=bias[:, o * 4 + t : o * 4 + t + 1],
                     )
 
-        def inter_t(b):
+        V_COLS = O * L - S_COLS
+
+        def group_s(b):
             t_grp[b] = work.tile([P, O * L * 4], BF16, name="t_grp", align_bytes=64)
+            if S_COLS:
+                nc.scalar.copy(
+                    out=t_grp[b][:, V_COLS * 4 :].rearrange("p (c i t) -> p c t i", i=4, t=4),
+                    in_=t_pl[b][:, :, V_COLS:].rearrange("p t (c i) -> p c t i", i=4),
+                )
+
+        def inter_t(b):
             nc.vector.tensor_copy(
-                out=t_grp[b][:].rearrange("p (c i t) -> p c t i", i=4, t=4),
-                in_=t_pl[b][:].rearrange("p t (c i) -> p c t i", i=4),
+                out=t_grp[b][:, 0 : V_COLS * 4].rearrange("p (c i t) -> p c t i", i=4, t=4),
+                in_=t_pl[b][:, :, 0:V_COLS].rearrange("p t (c i) -> p c t i", i=4),
             )
 
         def mm_out(b):
@@ -209,20 +221,20 @@ def tile_biaffine_pa_t_kernel(tc, x1, x2_bytes, x2_scale, bw, W_bil, t_ones, lin
                         out=o_bank[b, x][:, o * L : (o + 1) * L],
                         lhsT=t_c[b][:, o * L + x * P : o * L + (x + 1) * P].bitcast(FP8X4),
                         lhsT_scale=t_s[b][:, o * L + x * P : o * L + (x + 1) * P],
-                        rhs=x_c[b + 1][:, L : 2 * L].bitcast(FP8X4),
-                        rhs_scale=x_s[b + 1][:, L : 2 * L],
+                        rhs=x_c[b][:, L : 2 * L].bitcast(FP8X4),
+                        rhs_scale=x_s[b][:, L : 2 * L],
                         start=True,
                         stop=True,
                     )
 
-        def terms(b):
-            ra[b] = work.tile([P, 2, O, L], F32, name="ra", align_bytes=64)
+        def terms(b, x):
+            ra[b, x] = work.tile([P, O, L], F32, name=f"ra{x}", align_bytes=64)
             l2 = lin2_sb[b // LIN_GROUP][:, b % LIN_GROUP, :].rearrange("p (y o) -> p o y", o=2)
-            for x in range(2):
+            if True:
                 for o in range(O):
                     i = (x * B + b) * O + o
                     nc.gpsimd.tensor_scalar(
-                        out=ra[b][:, x, o, :], in0=l2[:, o, :], scalar1=bwn[:, 1:2], scalar2=a_sb[:, i : i + 1], op0=ALU.mult, op1=ALU.add
+                        out=ra[b, x][:, o, :], in0=l2[:, o, :], scalar1=bwn[:, 1:2], scalar2=a_sb[:, i : i + 1], op0=ALU.mult, op1=ALU.add
                     )
 
         def finish(b, x):
@@ -232,7 +244,7 @@ def tile_biaffine_pa_t_kernel(tc, x1, x2_bytes, x2_scale, bw, W_bil, t_ones, lin
                 out=o_sb[b][:, x, :].rearrange("p (y o) -> p y o", o=2),
                 in0=o_bank[b, x][:].rearrange("p (o y) -> p y o", o=2),
                 scalar=bwn[:, 0:1],
-                in1=ra[b][:, x].rearrange("p o y -> p y o"),
+                in1=ra[b, x][:].rearrange("p o y -> p y o"),
                 op0=ALU.mult,
                 op1=ALU.add,
             )
@@ -255,51 +267,64 @@ def tile_biaffine_pa_t_kernel(tc, x1, x2_bytes, x2_scale, bw, W_bil, t_ones, lin
         w_group(0, nc.vector.tensor_copy)
         tr_x1(0)
         evac_x1(0)
-        w_quant(0)
         cast_x2(0)
-        w_group(1, nc.scalar.copy)
         quant_x(0, 0, L)
+        w_quant(0)
         for x in range(2):
             nc.vector.tensor_tensor(out=tmp_v[:, x], in0=a_view[:, x, 32 : 32 + B], in1=blin_v, op=ALU.add)
         nc.vector.tensor_scalar(out=a_tmp[:], in0=a_tmp[:], scalar1=bwn[:, 1:2], scalar2=None, op0=ALU.mult)
-        w_quant(1)
+        w_group(1, nc.vector.tensor_copy)
         for x in range(2):
             nc.vector.scalar_tensor_tensor(
                 out=a_sb[:].rearrange("p (x b o) -> p x b o", x=2, o=2)[:, x],
                 in0=a_view[:, x, 0:B], scalar=bwn[:, 0:1], in1=tmp_v[:, x], op0=ALU.mult, op1=ALU.add,
             )
-        terms(0)
-        tr_x1(1)
         tr_x2(0)
+        tr_x1(1)
         evac_x1(1)
         cast_x2(1)
+        mm_t(0, 0)
+        evac_t(0, 0)
+        scale_x2(0)
+        w_quant(1)
+        quant_x(0, L, 2 * L)
+        for x in range(2):
+            terms(0, x)
+        tr_x2(1)
 
-        for s in range(B + 1):
+        for s in range(B + 3):
             if s < B:
-                mm_t(s)
-            if s >= 1:
-                mm_out(s - 1)
+                if s:
+                    mm_t(s, 0)
+                mm_t(s, 1)
             if s + 2 < B:
                 tr_x1(s + 2)
+            if 2 <= s <= B + 1:
+                mm_out(s - 2)
             if s < B:
-                evac_t(s)
+                if s:
+                    evac_t(s, 0)
+                evac_t(s, 1)
+            if s == 0:
+                cast_x2(2)
             if s + 2 < B:
                 evac_x1(s + 2)
-                cast_x2(s + 2)
+            if s < B:
+                group_s(s)
+            if s + 3 < B:
+                cast_x2(s + 3)
+            for x in range(2):
+                if s >= 3:
+                    finish(s - 3, x)
+                if s + 1 < B:
+                    terms(s + 1, x)
             if s + 1 < B:
-                terms(s + 1)
-            if s == B - 1:
-                x_grp[B] = work.tile([P, 2 * L * 4], BF16, name="x_grp", align_bytes=64)
-            if s < B:
-                scale_x2(s)
+                scale_x2(s + 1)
+            if s + 2 < B:
+                tr_x2(s + 2)
+            if 1 <= s <= B:
+                inter_t(s - 1)
             if s + 1 < B:
-                tr_x2(s + 1)
-            if s >= 1:
-                finish(s - 1, 0)
-            if s < B:
-                quant_x(s + 1, L if s == B - 1 else 0, 2 * L)
-                inter_t(s)
-            if s >= 1:
-                finish(s - 1, 1)
-            if s < B:
-                quant_t(s)
+                quant_x(s + 1, 0, 2 * L)
+            if 1 <= s <= B:
+                quant_t(s - 1)

from contextlib import ExitStack

import concourse.mybir as mybir
from concourse.masks import make_identity

B, L, D, O = 16, 256, 512, 2
FLOPS = 2 * D * (B * L) * (D * O) + 2 * B * L * L * D * O

F32 = mybir.dt.float32
BF16 = mybir.dt.bfloat16
U32 = mybir.dt.uint32
U8 = mybir.dt.uint8
FP8 = mybir.dt.float8_e4m3fn
FP8X4 = mybir.dt.float8_e4m3fn_x4
ACT = mybir.ActivationFunctionType
ALU = mybir.AluOpType
AX = mybir.AxisListType

P = 128
LIN_GROUP = 4
S_COLS = 128


def tile_biaffine_pa_t_kernel(tc, x1, x2_bytes, x2_scale, bw, W_bil, t_ones, lin1, lin2, b_lin, out):
    nc = tc.nc
    with ExitStack() as ctx:
        keep = ctx.enter_context(tc.tile_pool(name="keep", bufs=1))
        loads = ctx.enter_context(tc.tile_pool(name="loads", bufs=B))
        work = ctx.enter_context(tc.tile_pool(name="work", bufs=3))
        ps_tr = ctx.enter_context(tc.psum_pool(name="ps_tr", bufs=1))
        ps_t = ctx.enter_context(tc.psum_pool(name="ps_t", bufs=4))
        ps_o = ctx.enter_context(tc.psum_pool(name="ps_o", bufs=2))
        ctx.enter_context(tc.manual_schedule())

        w_raw = []
        for o in range(O):
            w_raw.append(keep.tile([P, 4, D], BF16, name=f"w_raw{o}", align_bytes=64))
        x1_sb, x2_sb = {}, {}

        def load_w(o):
            nc.sync.dma_start(out=w_raw[o][:], in_=W_bil[o, 0:D, :].rearrange("(p t) j -> p t j", t=4))

        def load_x1(b):
            x1_sb[b] = loads.tile([P, 2, D], BF16, name="x1_rows", align_bytes=64)
            nc.sync.dma_start(out=x1_sb[b][:], in_=x1[b].rearrange("(p x) k -> p x k", x=2))

        def load_x2(b):
            x2_sb[b] = loads.tile([P, 2, D], U8, name="x2_codes_in", align_bytes=64)
            nc.sync.dma_start(out=x2_sb[b][:], in_=x2_bytes[b].rearrange("(y p) k -> p y k", y=2))

        lin2_sb = {}

        def load_lin2(g):
            lin2_sb[g] = keep.tile([P, LIN_GROUP, L * O], BF16, name=f"lin2_{g}", align_bytes=64)
            nc.sync.dma_start(
                out=lin2_sb[g][:].rearrange("p b c -> p (b c)"),
                in_=lin2[g * LIN_GROUP : (g + 1) * LIN_GROUP].rearrange("b y o -> (b y o)").partition_broadcast(P),
            )

        load_x1(0)
        load_w(0)
        load_w(1)
        load_x2(0)
        load_x1(1)
        load_x2(1)
        load_x1(2)
        load_x2(2)
        load_lin2(0)
        for b in range(3, B):
            load_x1(b)
            load_x2(b)
            if b % LIN_GROUP == 1:
                load_lin2(b // LIN_GROUP)

        bw_sb = keep.tile([P, 2], BF16, name="bw_sb")
        nc.scalar.dma_start(out=bw_sb[:], in_=bw.partition_broadcast(P))
        scale_sb = keep.tile([P, 4], F32, name="scale_sb")
        nc.scalar.dma_start(out=scale_sb[:], in_=x2_scale.rearrange("a c (p t) -> p (a c t)", t=4))
        bias_bf = keep.tile([P, O, 4], BF16, name="bias_bf")
        nc.scalar.dma_start(out=bias_bf[:], in_=W_bil[:, D, :].rearrange("o (p t) -> p o t", t=4))
        blin_sb = keep.tile([P, 2], BF16, name="blin_sb")
        nc.scalar.dma_start(out=blin_sb[:], in_=b_lin.partition_broadcast(P))
        rows = keep.tile([P, L * O], BF16, name="rows")
        nc.gpsimd.memset(rows[:], 0.0)
        nc.scalar.dma_start(out=rows[0:B, :], in_=t_ones.rearrange("b x o -> b (x o)"))
        nc.scalar.dma_start(out=rows[32 : 32 + B, :], in_=lin1.rearrange("b x o -> b (x o)"))

        ident = keep.tile([P, P], F32, name="ident")
        make_identity(nc, ident[:])

        bw_max = keep.tile([P, 1], F32, name="bw_max")
        nc.vector.reduce_max(bw_max[:], bw_sb[:], axis=AX.X)
        bw_dif = keep.tile([P, 2], F32, name="bw_dif")
        nc.vector.tensor_scalar(out=bw_dif[:], in0=bw_sb[:], scalar1=bw_max[:], scalar2=None, op0=ALU.subtract)
        bw_exp = keep.tile([P, 2], F32, name="bw_exp")
        nc.scalar.activation(out=bw_exp[:], in_=bw_dif[:], func=ACT.Exp)
        bw_sum = keep.tile([P, 1], F32, name="bw_sum")
        nc.vector.reduce_sum(bw_sum[:], bw_exp[:], axis=AX.X)
        bw_inv = keep.tile([P, 1], F32, name="bw_inv")
        nc.vector.reciprocal(out=bw_inv[:], in_=bw_sum[:])
        bwn = keep.tile([P, 2], F32, name="bwn")
        nc.vector.tensor_scalar(out=bwn[:], in0=bw_exp[:], scalar1=bw_inv[:], scalar2=None, op0=ALU.mult)
        bias = keep.tile([P, O * 4], F32, name="bias")
        nc.vector.tensor_copy(out=bias[:], in_=bias_bf[:].rearrange("p o t -> p (o t)"))

        w_codes, w_scales = [], []
        w_grp = []
        for o in range(O):
            w_grp.append(keep.tile([P, D * 4], BF16, name=f"w_grp{o}", align_bytes=64))
            w_codes.append(keep.tile([P, D], U32, name=f"w_codes{o}", align_bytes=64))
            w_scales.append(keep.tile([P, D], U8, name=f"w_scales{o}", align_bytes=64))

        def w_group(o, copy):
            for t in range(4):
                copy(
                    out=w_grp[o][:].rearrange("p (t m j) -> p t m j", t=4, j=4)[:, t],
                    in_=w_raw[o][:].rearrange("p j (m t) -> p t m j", t=4)[:, t],
                )

        def w_quant(o):
            nc.vector.quantize_mx(out=w_codes[o][:].bitcast(FP8X4), scales=w_scales[o][:], in_=w_grp[o][:])

        x2_bf, x1_tr, x2_tr, x_grp = {}, {}, {}, {}
        x_c, x_s, t_bank, t_pl, t_grp, t_c, t_s, o_bank, ra, o_sb = {}, {}, {}, {}, {}, {}, {}, {}, {}, {}

        def cast_x2(b):
            x2_bf[b] = work.tile([P, 2, D], BF16, name="x2_bf", bufs=4, align_bytes=64)
            nc.scalar.copy(out=x2_bf[b][:], in_=x2_sb[b][:].bitcast(FP8))

        def transpose_rows(src, dst):
            words = src[:].rearrange("p x k -> p (x k)").bitcast(F32)
            for x in range(2):
                for u in range(2):
                    nc.tensor.transpose(
                        dst[:, (2 * u + x) * P : (2 * u + x + 1) * P],
                        words[:, x * 256 + u : (x + 1) * 256 : 2],
                        ident[:],
                    )

        def tr_x1(b):
            x1_tr[b] = ps_tr.tile([P, 512], F32, name="x1_tr")
            transpose_rows(x1_sb[b], x1_tr[b])

        def tr_x2(b):
            x2_tr[b] = ps_tr.tile([P, 512], F32, name="x2_tr")
            transpose_rows(x2_bf[b], x2_tr[b])

        def evac_x1(b):
            x_grp[b] = work.tile([P, 2 * L * 4], BF16, name="x_grp", align_bytes=64)
            nc.scalar.copy(
                out=x_grp[b][:, 0 : L * 4].bitcast(F32).rearrange("p (c u) -> p c u", u=2),
                in_=x1_tr[b][:].rearrange("p (u c) -> p c u", u=2),
            )

        def quant_x(b, lo, hi):
            if lo == 0:
                x_c[b] = work.tile([P, 2 * L], U32, name="x_c", bufs=4, align_bytes=64)
                x_s[b] = work.tile([P, 2 * L], U8, name="x_s", bufs=4, align_bytes=64)
            nc.vector.quantize_mx(out=x_c[b][:, lo:hi].bitcast(FP8X4), scales=x_s[b][:, lo:hi], in_=x_grp[b][:, 4 * lo : 4 * hi])

        def quant_t(b):
            t_c[b] = work.tile([P, 2 * L], U32, name="t_c", align_bytes=64)
            t_s[b] = work.tile([P, 2 * L], U8, name="t_s", align_bytes=64)
            nc.vector.quantize_mx(out=t_c[b][:].bitcast(FP8X4), scales=t_s[b][:], in_=t_grp[b][:])

        def scale_x2(b):
            src = x2_tr[b][:].bitcast(BF16).rearrange("p (u c e) -> p c u e", u=2, e=2)
            dst = x_grp[b][:, L * 4 :].rearrange("p (c u e) -> p c u e", u=2, e=2)
            sc = scale_sb[:].rearrange("p (u e) -> p u e", e=2).unsqueeze(1).to_broadcast([P, L, 2, 2])
            nc.vector.tensor_tensor(out=dst, in0=src, in1=sc, op=ALU.mult)

        def mm_t(b, o):
            if o == 0:
                t_pl[b] = work.tile([P, 4, O * L], BF16, name="t_pl", align_bytes=64)
            if True:
                for h in range(2):
                    bank = ps_t.tile([P, 512], F32, name="t_bank")
                    t_bank[b, o, h] = bank
                    for t in (2 * h, 2 * h + 1):
                        nc.tensor.matmul_mx(
                            out=bank[:, (t % 2) * L : (t % 2 + 1) * L],
                            lhsT=w_codes[o][:, t * P : (t + 1) * P].bitcast(FP8X4),
                            lhsT_scale=w_scales[o][:, t * P : (t + 1) * P],
                            rhs=x_c[b][:, 0:L].bitcast(FP8X4),
                            rhs_scale=x_s[b][:, 0:L],
                            start=True,
                            stop=True,
                        )

        def evac_t(b, o):
            if True:
                for t in range(4):
                    nc.scalar.activation(
                        out=t_pl[b][:, t, o * L : (o + 1) * L],
                        in_=t_bank[b, o, t // 2][:, (t % 2) * L : (t % 2 + 1) * L],
                        func=ACT.Identity,
                        bias=bias[:, o * 4 + t : o * 4 + t + 1],
                    )

        V_COLS = O * L - S_COLS

        def group_s(b):
            t_grp[b] = work.tile([P, O * L * 4], BF16, name="t_grp", align_bytes=64)
            if S_COLS:
                nc.scalar.copy(
                    out=t_grp[b][:, V_COLS * 4 :].rearrange("p (c i t) -> p c t i", i=4, t=4),
                    in_=t_pl[b][:, :, V_COLS:].rearrange("p t (c i) -> p c t i", i=4),
                )

        def inter_t(b):
            nc.vector.tensor_copy(
                out=t_grp[b][:, 0 : V_COLS * 4].rearrange("p (c i t) -> p c t i", i=4, t=4),
                in_=t_pl[b][:, :, 0:V_COLS].rearrange("p t (c i) -> p c t i", i=4),
            )

        def mm_out(b):
            for x in range(2):
                o_bank[b, x] = ps_o.tile([P, 512], F32, name="o_bank")
                for o in range(O):
                    nc.tensor.matmul_mx(
                        out=o_bank[b, x][:, o * L : (o + 1) * L],
                        lhsT=t_c[b][:, o * L + x * P : o * L + (x + 1) * P].bitcast(FP8X4),
                        lhsT_scale=t_s[b][:, o * L + x * P : o * L + (x + 1) * P],
                        rhs=x_c[b][:, L : 2 * L].bitcast(FP8X4),
                        rhs_scale=x_s[b][:, L : 2 * L],
                        start=True,
                        stop=True,
                    )

        def terms(b, x):
            ra[b, x] = work.tile([P, O, L], F32, name=f"ra{x}", align_bytes=64)
            l2 = lin2_sb[b // LIN_GROUP][:, b % LIN_GROUP, :].rearrange("p (y o) -> p o y", o=2)
            if True:
                for o in range(O):
                    i = (x * B + b) * O + o
                    nc.gpsimd.tensor_scalar(
                        out=ra[b, x][:, o, :], in0=l2[:, o, :], scalar1=bwn[:, 1:2], scalar2=a_sb[:, i : i + 1], op0=ALU.mult, op1=ALU.add
                    )

        def finish(b, x):
            if x == 0:
                o_sb[b] = work.tile([P, 2, L * O], F32, name="o_sb", align_bytes=64)
            nc.vector.scalar_tensor_tensor(
                out=o_sb[b][:, x, :].rearrange("p (y o) -> p y o", o=2),
                in0=o_bank[b, x][:].rearrange("p (o y) -> p y o", o=2),
                scalar=bwn[:, 0:1],
                in1=ra[b, x][:].rearrange("p o y -> p y o"),
                op0=ALU.mult,
                op1=ALU.add,
            )
            dst = out[b].rearrange("(p x) y o -> p x (y o)", x=2)
            if b == B - 1:
                nc.sync.dma_start(out=dst[:, x, :], in_=o_sb[b][:, x, :])
            elif x == 1:
                nc.sync.dma_start(out=dst, in_=o_sb[b][:])

        a_tr = ps_o.tile([P, 512], F32, name="o_bank")
        a_words = rows[:].bitcast(F32)
        for x in range(2):
            nc.tensor.transpose(a_tr[:, x * P : (x + 1) * P], a_words[:, x::2], ident[:])
        a_sb = keep.tile([P, 2 * B * O], F32, name="a_sb")
        a_tmp = keep.tile([P, 2 * B * O], F32, name="a_tmp")
        a_view = a_tr[:, 0 : 2 * P].bitcast(BF16).rearrange("p (x w o) -> p x w o", x=2, o=2)
        tmp_v = a_tmp[:].rearrange("p (x b o) -> p x b o", x=2, o=2)
        blin_v = blin_sb[:].unsqueeze(1).to_broadcast([P, B, O])

        w_group(0, nc.vector.tensor_copy)
        tr_x1(0)
        evac_x1(0)
        cast_x2(0)
        quant_x(0, 0, L)
        w_quant(0)
        for x in range(2):
            nc.vector.tensor_tensor(out=tmp_v[:, x], in0=a_view[:, x, 32 : 32 + B], in1=blin_v, op=ALU.add)
        nc.vector.tensor_scalar(out=a_tmp[:], in0=a_tmp[:], scalar1=bwn[:, 1:2], scalar2=None, op0=ALU.mult)
        w_group(1, nc.vector.tensor_copy)
        for x in range(2):
            nc.vector.scalar_tensor_tensor(
                out=a_sb[:].rearrange("p (x b o) -> p x b o", x=2, o=2)[:, x],
                in0=a_view[:, x, 0:B], scalar=bwn[:, 0:1], in1=tmp_v[:, x], op0=ALU.mult, op1=ALU.add,
            )
        tr_x2(0)
        tr_x1(1)
        evac_x1(1)
        cast_x2(1)
        mm_t(0, 0)
        evac_t(0, 0)
        scale_x2(0)
        w_quant(1)
        quant_x(0, L, 2 * L)
        for x in range(2):
            terms(0, x)
        tr_x2(1)

        for s in range(B + 3):
            if s < B:
                if s:
                    mm_t(s, 0)
                mm_t(s, 1)
            if s + 2 < B:
                tr_x1(s + 2)
            if 2 <= s <= B + 1:
                mm_out(s - 2)
            if s < B:
                if s:
                    evac_t(s, 0)
                evac_t(s, 1)
            if s == 0:
                cast_x2(2)
            if s + 2 < B:
                evac_x1(s + 2)
            if s < B:
                group_s(s)
            if s + 3 < B:
                cast_x2(s + 3)
            for x in range(2):
                if s >= 3:
                    finish(s - 3, x)
                if s + 1 < B:
                    terms(s + 1, x)
            if s + 1 < B:
                scale_x2(s + 1)
            if s + 2 < B:
                tr_x2(s + 2)
            if 1 <= s <= B:
                inter_t(s - 1)
            if s + 1 < B:
                quant_x(s + 1, 0, 2 * L)
            if 1 <= s <= B:
                quant_t(s - 1)
